import numpy as np
import ml_dtypes

BF16 = ml_dtypes.bfloat16


def bf(x):
    return np.asarray(x, np.float32).astype(BF16)


def f32(x):
    return np.asarray(x, np.float32)


def f64(x):
    return np.asarray(x).astype(np.float64)


def striped(idx):
    return np.tile(idx.reshape(-1, 16).T, (8, 1))


K, E, S, N = 1024, 128, 256, 128


def setup_inputs():
    return {"x": bf(0.25 * np.random.standard_normal((E, N))), "centers": bf(0.15 * np.random.standard_normal((E, K))), "u": f32(np.random.uniform(0.01, 0.99, (K, N))), "base": f32(3.0 * np.random.standard_normal((K, S))), "offs": striped(np.random.permutation(S)[:N])}


def reference(x, centers, u, base, offs):
    idx = offs[:16].T.reshape(-1)
    xx = f64(x)
    cc = f64(centers)
    x2 = np.sum(xx * xx, axis=0)[None, :]
    c2 = np.sum(cc * cc, axis=0)[:, None]
    negd = 2.0 * (cc.T @ xx) - x2 - c2
    noise = -np.log(-np.log(f64(u)))
    res = f64(base).copy()
    res[:, idx] = negd + noise
    return res

@@ -1,0 +1,63 @@
+import concourse.mybir as mybir
+
+K, E, S, N = 1024, 128, 256, 128
+P = 128
+BLOCKS = K // P
+FLOPS = 2 * K * E * N
+
+F32, BF16, U16 = mybir.dt.float32, mybir.dt.bfloat16, mybir.dt.uint16
+ADD = mybir.AluOpType.add
+LN = mybir.ActivationFunctionType.Ln
+
+
+def tile_softclusteringmodule_kernel(tc, x, centers, u, base, offs, out):
+    nc = tc.nc
+    with (
+        tc.tile_pool(name="held", bufs=1) as held,
+        tc.tile_pool(name="blocks", bufs=BLOCKS) as blocks,
+        tc.psum_pool(name="banks", bufs=BLOCKS) as banks,
+    ):
+        offsets = held.tile([P, N // 16], U16, name="offsets")
+        nc.sync.dma_start(offsets[:], offs)
+        x_sb = held.tile([E, N], BF16, name="x_sb")
+        nc.sync.dma_start(x_sb[:], x)
+        centers_sb = held.tile([E, K], BF16, name="centers_sb")
+        nc.sync.dma_start(centers_sb[:], centers)
+        windows = []
+        noises = []
+        for b in range(BLOCKS):
+            rows = slice(b * P, (b + 1) * P)
+            noise = blocks.tile([P, N], F32, name="noise")
+            nc.scalar.dma_start(noise[:], u[rows, :])
+            noises.append(noise)
+            window = blocks.tile([P, S], F32, name="window")
+            nc.sync.dma_start(window[:], base[rows, :])
+            windows.append(window)
+
+        minus_ones = held.tile([E, P], BF16, name="minus_ones")
+        nc.vector.memset(minus_ones[:], -1.0)
+        twice_x = held.tile([E, N], BF16, name="twice_x")
+        nc.vector.tensor_scalar_mul(twice_x[:], x_sb[:], 2.0)
+        x_squared = held.tile([E, N], BF16, name="x_squared")
+        nc.vector.tensor_mul(x_squared[:], x_sb[:], x_sb[:])
+        centers_squared = held.tile([E, K], BF16, name="centers_squared")
+        nc.vector.tensor_mul(centers_squared[:], centers_sb[:], centers_sb[:])
+
+        for b in range(BLOCKS):
+            rows = slice(b * P, (b + 1) * P)
+            noise, window = noises[b], windows[b]
+
+            nc.scalar.activation(noise[:], noise[:], LN)
+            nc.scalar.activation(noise[:], noise[:], LN, scale=-1.0)
+            nc.scalar.mul(noise[:], noise[:], -1.0)
+
+            negd = banks.tile([P, N], F32, name="negd")
+            nc.tensor.matmul(negd[:], centers_sb[:, rows], twice_x[:], start=True, stop=False)
+            nc.tensor.matmul(negd[:], minus_ones[:], x_squared[:], start=False, stop=False)
+            nc.tensor.matmul(negd[:], centers_squared[:, rows], minus_ones[:], start=False, stop=True)
+
+            negd_sb = blocks.tile([P, N], F32, name="negd_sb")
+            nc.scalar.copy(negd_sb[:], negd[:])
+
+            nc.vector.tensor_tensor(window[:].indirect(offsets[:]), negd_sb[:], noise[:], ADD)
+            nc.sync.dma_start(out[rows, :], window[:])

@@ -34,6 +34,10 @@ def tile_softclusteringmodule_kernel(tc, x, centers, u, base, offs, out):
             nc.sync.dma_start(window[:], base[rows, :])
             windows.append(window)
 
+        warm = held.tile([P, 1], F32, name="warm")
+        nc.gpsimd.memset(warm[:], 1.0)
+        nc.scalar.activation(warm[:], warm[:], LN)
+
         minus_ones = held.tile([E, P], BF16, name="minus_ones")
         nc.vector.memset(minus_ones[:], -1.0)
         twice_x = held.tile([E, N], BF16, name="twice_x")

@@ -3,6 +3,7 @@ import concourse.mybir as mybir
 K, E, S, N = 1024, 128, 256, 128
 P = 128
 BLOCKS = K // P
+PAIR = 2
 FLOPS = 2 * K * E * N
 
 F32, BF16, U16 = mybir.dt.float32, mybir.dt.bfloat16, mybir.dt.uint16
@@ -14,29 +15,27 @@ def tile_softclusteringmodule_kernel(tc, x, centers, u, base, offs, out):
     nc = tc.nc
     with (
         tc.tile_pool(name="held", bufs=1) as held,
+        tc.tile_pool(name="pairs", bufs=BLOCKS // PAIR) as pairs,
         tc.tile_pool(name="blocks", bufs=BLOCKS) as blocks,
         tc.psum_pool(name="banks", bufs=BLOCKS) as banks,
     ):
+        x_sb = held.tile([E, N], BF16, name="x_sb")
+        nc.scalar.dma_start(x_sb[:], x)
+        centers_sb = held.tile([E, K], BF16, name="centers_sb")
+        nc.scalar.dma_start(centers_sb[:], centers)
+        noise_pairs = []
+        for g in range(BLOCKS // PAIR):
+            noise_pair = pairs.tile([P, PAIR, N], F32, name="noise_pair")
+            u_pair = u[g * PAIR * P : (g + 1) * PAIR * P, :]
+            nc.sync.dma_start(noise_pair[:], u_pair.rearrange("(i p) j -> p i j", p=P))
+            noise_pairs.append(noise_pair)
         offsets = held.tile([P, N // 16], U16, name="offsets")
         nc.sync.dma_start(offsets[:], offs)
-        x_sb = held.tile([E, N], BF16, name="x_sb")
-        nc.sync.dma_start(x_sb[:], x)
-        centers_sb = held.tile([E, K], BF16, name="centers_sb")
-        nc.sync.dma_start(centers_sb[:], centers)
         windows = []
-        noises = []
         for b in range(BLOCKS):
-            rows = slice(b * P, (b + 1) * P)
-            noise = blocks.tile([P, N], F32, name="noise")
-            nc.scalar.dma_start(noise[:], u[rows, :])
-            noises.append(noise)
             window = blocks.tile([P, S], F32, name="window")
-            nc.sync.dma_start(window[:], base[rows, :])
+            nc.sync.dma_start(window[:], base[b * P : (b + 1) * P, :])
             windows.append(window)
-
-        warm = held.tile([P, 1], F32, name="warm")
-        nc.gpsimd.memset(warm[:], 1.0)
-        nc.scalar.activation(warm[:], warm[:], LN)
 
         minus_ones = held.tile([E, P], BF16, name="minus_ones")
         nc.vector.memset(minus_ones[:], -1.0)
@@ -44,24 +43,28 @@ def tile_softclusteringmodule_kernel(tc, x, centers, u, base, offs, out):
         nc.vector.tensor_scalar_mul(twice_x[:], x_sb[:], 2.0)
         x_squared = held.tile([E, N], BF16, name="x_squared")
         nc.vector.tensor_mul(x_squared[:], x_sb[:], x_sb[:])
-        centers_squared = held.tile([E, K], BF16, name="centers_squared")
-        nc.vector.tensor_mul(centers_squared[:], centers_sb[:], centers_sb[:])
+        squares = []
+        for b in range(BLOCKS):
+            rows = slice(b * P, (b + 1) * P)
+            centers_squared = blocks.tile([E, P], BF16, name="centers_squared")
+            nc.vector.tensor_mul(centers_squared[:], centers_sb[:, rows], centers_sb[:, rows])
+            squares.append(centers_squared)
 
         for b in range(BLOCKS):
             rows = slice(b * P, (b + 1) * P)
-            noise, window = noises[b], windows[b]
+            noise = noise_pairs[b // PAIR][:, b % PAIR, :]
+            window = windows[b]
 
-            nc.scalar.activation(noise[:], noise[:], LN)
-            nc.scalar.activation(noise[:], noise[:], LN, scale=-1.0)
-            nc.scalar.mul(noise[:], noise[:], -1.0)
+            nc.scalar.activation(noise, noise, LN)
+            nc.scalar.activation(noise, noise, LN, scale=-1.0)
+            nc.scalar.mul(noise, noise, -1.0)
 
             negd = banks.tile([P, N], F32, name="negd")
             nc.tensor.matmul(negd[:], centers_sb[:, rows], twice_x[:], start=True, stop=False)
             nc.tensor.matmul(negd[:], minus_ones[:], x_squared[:], start=False, stop=False)
-            nc.tensor.matmul(negd[:], centers_squared[:, rows], minus_ones[:], start=False, stop=True)
-
+            nc.tensor.matmul(negd[:], squares[b][:], minus_ones[:], start=False, stop=True)
             negd_sb = blocks.tile([P, N], F32, name="negd_sb")
             nc.scalar.copy(negd_sb[:], negd[:])
 
-            nc.vector.tensor_tensor(window[:].indirect(offsets[:]), negd_sb[:], noise[:], ADD)
+            nc.vector.tensor_tensor(window[:].indirect(offsets[:]), negd_sb[:], noise, ADD)
             nc.sync.dma_start(out[rows, :], window[:])

@@ -23,19 +23,19 @@ def tile_softclusteringmodule_kernel(tc, x, centers, u, base, offs, out):
         nc.scalar.dma_start(x_sb[:], x)
         centers_sb = held.tile([E, K], BF16, name="centers_sb")
         nc.scalar.dma_start(centers_sb[:], centers)
+        offsets = held.tile([P, N // 16], U16, name="offsets")
+        nc.sync.dma_start(offsets[:], offs)
         noise_pairs = []
+        windows = []
         for g in range(BLOCKS // PAIR):
             noise_pair = pairs.tile([P, PAIR, N], F32, name="noise_pair")
             u_pair = u[g * PAIR * P : (g + 1) * PAIR * P, :]
             nc.sync.dma_start(noise_pair[:], u_pair.rearrange("(i p) j -> p i j", p=P))
             noise_pairs.append(noise_pair)
-        offsets = held.tile([P, N // 16], U16, name="offsets")
-        nc.sync.dma_start(offsets[:], offs)
-        windows = []
-        for b in range(BLOCKS):
-            window = blocks.tile([P, S], F32, name="window")
-            nc.sync.dma_start(window[:], base[b * P : (b + 1) * P, :])
-            windows.append(window)
+            for b in range(g * PAIR, (g + 1) * PAIR):
+                window = blocks.tile([P, S], F32, name="window")
+                nc.sync.dma_start(window[:], base[b * P : (b + 1) * P, :])
+                windows.append(window)
 
         minus_ones = held.tile([E, P], BF16, name="minus_ones")
         nc.vector.memset(minus_ones[:], -1.0)

@@ -4,6 +4,7 @@ K, E, S, N = 1024, 128, 256, 128
 P = 128
 BLOCKS = K // P
 PAIR = 2
+HALF = BLOCKS // 2
 FLOPS = 2 * K * E * N
 
 F32, BF16, U16 = mybir.dt.float32, mybir.dt.bfloat16, mybir.dt.uint16
@@ -15,14 +16,18 @@ def tile_softclusteringmodule_kernel(tc, x, centers, u, base, offs, out):
     nc = tc.nc
     with (
         tc.tile_pool(name="held", bufs=1) as held,
+        tc.tile_pool(name="halves", bufs=BLOCKS // HALF) as halves,
         tc.tile_pool(name="pairs", bufs=BLOCKS // PAIR) as pairs,
         tc.tile_pool(name="blocks", bufs=BLOCKS) as blocks,
         tc.psum_pool(name="banks", bufs=BLOCKS) as banks,
     ):
         x_sb = held.tile([E, N], BF16, name="x_sb")
         nc.scalar.dma_start(x_sb[:], x)
-        centers_sb = held.tile([E, K], BF16, name="centers_sb")
-        nc.scalar.dma_start(centers_sb[:], centers)
+        centers_blocks = []
+        for h in range(BLOCKS // HALF):
+            centers_half = halves.tile([E, HALF * P], BF16, name="centers_half")
+            nc.scalar.dma_start(centers_half[:], centers[:, h * HALF * P : (h + 1) * HALF * P])
+            centers_blocks += [centers_half[:, i * P : (i + 1) * P] for i in range(HALF)]
         offsets = held.tile([P, N // 16], U16, name="offsets")
         nc.sync.dma_start(offsets[:], offs)
         noise_pairs = []
@@ -45,9 +50,8 @@ def tile_softclusteringmodule_kernel(tc, x, centers, u, base, offs, out):
         nc.vector.tensor_mul(x_squared[:], x_sb[:], x_sb[:])
         squares = []
         for b in range(BLOCKS):
-            rows = slice(b * P, (b + 1) * P)
             centers_squared = blocks.tile([E, P], BF16, name="centers_squared")
-            nc.vector.tensor_mul(centers_squared[:], centers_sb[:, rows], centers_sb[:, rows])
+            nc.vector.tensor_mul(centers_squared[:], centers_blocks[b], centers_blocks[b])
             squares.append(centers_squared)
 
         for b in range(BLOCKS):
@@ -60,8 +64,8 @@ def tile_softclusteringmodule_kernel(tc, x, centers, u, base, offs, out):
             nc.scalar.mul(noise, noise, -1.0)
 
             negd = banks.tile([P, N], F32, name="negd")
-            nc.tensor.matmul(negd[:], centers_sb[:, rows], twice_x[:], start=True, stop=False)
-            nc.tensor.matmul(negd[:], minus_ones[:], x_squared[:], start=False, stop=False)
+            nc.tensor.matmul(negd[:], minus_ones[:], x_squared[:], start=True, stop=False)
+            nc.tensor.matmul(negd[:], centers_blocks[b], twice_x[:], start=False, stop=False)
             nc.tensor.matmul(negd[:], squares[b][:], minus_ones[:], start=False, stop=True)
             negd_sb = blocks.tile([P, N], F32, name="negd_sb")
             nc.scalar.copy(negd_sb[:], negd[:])

@@ -19,7 +19,7 @@ def tile_softclusteringmodule_kernel(tc, x, centers, u, base, offs, out):
         tc.tile_pool(name="halves", bufs=BLOCKS // HALF) as halves,
         tc.tile_pool(name="pairs", bufs=BLOCKS // PAIR) as pairs,
         tc.tile_pool(name="blocks", bufs=BLOCKS) as blocks,
-        tc.psum_pool(name="banks", bufs=BLOCKS) as banks,
+        tc.psum_pool(name="banks", bufs=2) as banks,
     ):
         x_sb = held.tile([E, N], BF16, name="x_sb")
         nc.scalar.dma_start(x_sb[:], x)
@@ -29,7 +29,6 @@ def tile_softclusteringmodule_kernel(tc, x, centers, u, base, offs, out):
             nc.scalar.dma_start(centers_half[:], centers[:, h * HALF * P : (h + 1) * HALF * P])
             centers_blocks += [centers_half[:, i * P : (i + 1) * P] for i in range(HALF)]
         offsets = held.tile([P, N // 16], U16, name="offsets")
-        nc.sync.dma_start(offsets[:], offs)
         noise_pairs = []
         windows = []
         for g in range(BLOCKS // PAIR):
@@ -37,6 +36,8 @@ def tile_softclusteringmodule_kernel(tc, x, centers, u, base, offs, out):
             u_pair = u[g * PAIR * P : (g + 1) * PAIR * P, :]
             nc.sync.dma_start(noise_pair[:], u_pair.rearrange("(i p) j -> p i j", p=P))
             noise_pairs.append(noise_pair)
+            if g == 0:
+                nc.sync.dma_start(offsets[:], offs)
             for b in range(g * PAIR, (g + 1) * PAIR):
                 window = blocks.tile([P, S], F32, name="window")
                 nc.sync.dma_start(window[:], base[b * P : (b + 1) * P, :])

@@ -5,6 +5,7 @@ P = 128
 BLOCKS = K // P
 PAIR = 2
 HALF = BLOCKS // 2
+AHEAD = 2
 FLOPS = 2 * K * E * N
 
 F32, BF16, U16 = mybir.dt.float32, mybir.dt.bfloat16, mybir.dt.uint16
@@ -31,11 +32,17 @@ def tile_softclusteringmodule_kernel(tc, x, centers, u, base, offs, out):
         offsets = held.tile([P, N // 16], U16, name="offsets")
         noise_pairs = []
         windows = []
-        for g in range(BLOCKS // PAIR):
+
+        def load_u_pair(g):
             noise_pair = pairs.tile([P, PAIR, N], F32, name="noise_pair")
             u_pair = u[g * PAIR * P : (g + 1) * PAIR * P, :]
             nc.sync.dma_start(noise_pair[:], u_pair.rearrange("(i p) j -> p i j", p=P))
             noise_pairs.append(noise_pair)
+
+        load_u_pair(0)
+        for g in range(BLOCKS // PAIR):
+            if g + 1 < BLOCKS // PAIR:
+                load_u_pair(g + 1)
             if g == 0:
                 nc.sync.dma_start(offsets[:], offs)
             for b in range(g * PAIR, (g + 1) * PAIR):
@@ -55,14 +62,21 @@ def tile_softclusteringmodule_kernel(tc, x, centers, u, base, offs, out):
             nc.vector.tensor_mul(centers_squared[:], centers_blocks[b], centers_blocks[b])
             squares.append(centers_squared)
 
+        def make_noise(b):
+            noise = noise_pairs[b // PAIR][:, b % PAIR, :]
+            nc.scalar.activation(noise, noise, LN)
+            nc.scalar.activation(noise, noise, LN, scale=-1.0)
+            nc.scalar.mul(noise, noise, -1.0)
+
+        for b in range(AHEAD):
+            make_noise(b)
+
         for b in range(BLOCKS):
             rows = slice(b * P, (b + 1) * P)
             noise = noise_pairs[b // PAIR][:, b % PAIR, :]
             window = windows[b]
-
-            nc.scalar.activation(noise, noise, LN)
-            nc.scalar.activation(noise, noise, LN, scale=-1.0)
-            nc.scalar.mul(noise, noise, -1.0)
+            if b + AHEAD < BLOCKS:
+                make_noise(b + AHEAD)
 
             negd = banks.tile([P, N], F32, name="negd")
             nc.tensor.matmul(negd[:], minus_ones[:], x_squared[:], start=True, stop=False)

@@ -4,7 +4,6 @@ K, E, S, N = 1024, 128, 256, 128
 P = 128
 BLOCKS = K // P
 PAIR = 2
-HALF = BLOCKS // 2
 AHEAD = 2
 FLOPS = 2 * K * E * N
 
@@ -17,18 +16,18 @@ def tile_softclusteringmodule_kernel(tc, x, centers, u, base, offs, out):
     nc = tc.nc
     with (
         tc.tile_pool(name="held", bufs=1) as held,
-        tc.tile_pool(name="halves", bufs=BLOCKS // HALF) as halves,
         tc.tile_pool(name="pairs", bufs=BLOCKS // PAIR) as pairs,
         tc.tile_pool(name="blocks", bufs=BLOCKS) as blocks,
         tc.psum_pool(name="banks", bufs=2) as banks,
     ):
         x_sb = held.tile([E, N], BF16, name="x_sb")
         nc.scalar.dma_start(x_sb[:], x)
-        centers_blocks = []
-        for h in range(BLOCKS // HALF):
-            centers_half = halves.tile([E, HALF * P], BF16, name="centers_half")
-            nc.scalar.dma_start(centers_half[:], centers[:, h * HALF * P : (h + 1) * HALF * P])
-            centers_blocks += [centers_half[:, i * P : (i + 1) * P] for i in range(HALF)]
+        centers_first = held.tile([E, PAIR * P], BF16, name="centers_first")
+        nc.scalar.dma_start(centers_first[:], centers[:, : PAIR * P])
+        centers_rest = held.tile([E, K - PAIR * P], BF16, name="centers_rest")
+        nc.scalar.dma_start(centers_rest[:], centers[:, PAIR * P :])
+        centers_blocks = [centers_first[:, i * P : (i + 1) * P] for i in range(PAIR)]
+        centers_blocks += [centers_rest[:, i * P : (i + 1) * P] for i in range(BLOCKS - PAIR)]
         offsets = held.tile([P, N // 16], U16, name="offsets")
         noise_pairs = []
         windows = []
@@ -62,21 +61,21 @@ def tile_softclusteringmodule_kernel(tc, x, centers, u, base, offs, out):
             nc.vector.tensor_mul(centers_squared[:], centers_blocks[b], centers_blocks[b])
             squares.append(centers_squared)
 
-        def make_noise(b):
+        def take_logs(b):
             noise = noise_pairs[b // PAIR][:, b % PAIR, :]
             nc.scalar.activation(noise, noise, LN)
             nc.scalar.activation(noise, noise, LN, scale=-1.0)
-            nc.scalar.mul(noise, noise, -1.0)
 
         for b in range(AHEAD):
-            make_noise(b)
+            take_logs(b)
 
         for b in range(BLOCKS):
             rows = slice(b * P, (b + 1) * P)
             noise = noise_pairs[b // PAIR][:, b % PAIR, :]
             window = windows[b]
             if b + AHEAD < BLOCKS:
-                make_noise(b + AHEAD)
+                take_logs(b + AHEAD)
+            nc.scalar.mul(noise, noise, -1.0)
 
             negd = banks.tile([P, N], F32, name="negd")
             nc.tensor.matmul(negd[:], minus_ones[:], x_squared[:], start=True, stop=False)

@@ -3,8 +3,9 @@ import concourse.mybir as mybir
 K, E, S, N = 1024, 128, 256, 128
 P = 128
 BLOCKS = K // P
-PAIR = 2
-AHEAD = 2
+U_LOADS = (1, 1, 2, 4)
+AHEAD = 1
+FIRST = P
 FLOPS = 2 * K * E * N
 
 F32, BF16, U16 = mybir.dt.float32, mybir.dt.bfloat16, mybir.dt.uint16
@@ -16,73 +17,80 @@ def tile_softclusteringmodule_kernel(tc, x, centers, u, base, offs, out):
     nc = tc.nc
     with (
         tc.tile_pool(name="held", bufs=1) as held,
-        tc.tile_pool(name="pairs", bufs=BLOCKS // PAIR) as pairs,
         tc.tile_pool(name="blocks", bufs=BLOCKS) as blocks,
+        tc.tile_pool(name="ring", bufs=AHEAD + 1) as ring,
         tc.psum_pool(name="banks", bufs=2) as banks,
     ):
         x_sb = held.tile([E, N], BF16, name="x_sb")
-        nc.scalar.dma_start(x_sb[:], x)
-        centers_first = held.tile([E, PAIR * P], BF16, name="centers_first")
-        nc.scalar.dma_start(centers_first[:], centers[:, : PAIR * P])
-        centers_rest = held.tile([E, K - PAIR * P], BF16, name="centers_rest")
-        nc.scalar.dma_start(centers_rest[:], centers[:, PAIR * P :])
-        centers_blocks = [centers_first[:, i * P : (i + 1) * P] for i in range(PAIR)]
-        centers_blocks += [centers_rest[:, i * P : (i + 1) * P] for i in range(BLOCKS - PAIR)]
+        centers_first = held.tile([E, FIRST], BF16, name="centers_first")
+        centers_rest = held.tile([E, K - FIRST], BF16, name="centers_rest")
         offsets = held.tile([P, N // 16], U16, name="offsets")
-        noise_pairs = []
+        u_blocks = []
         windows = []
 
-        def load_u_pair(g):
-            noise_pair = pairs.tile([P, PAIR, N], F32, name="noise_pair")
-            u_pair = u[g * PAIR * P : (g + 1) * PAIR * P, :]
-            nc.sync.dma_start(noise_pair[:], u_pair.rearrange("(i p) j -> p i j", p=P))
-            noise_pairs.append(noise_pair)
+        def load_u(size):
+            u_tile = held.tile([P, size, N], F32, name=f"u_{len(u_blocks)}")
+            rows = u[len(u_blocks) * P : (len(u_blocks) + size) * P, :]
+            nc.sync.dma_start(u_tile[:], rows.rearrange("(i p) j -> p i j", p=P))
+            u_blocks.extend([u_tile[:, i, :] for i in range(size)])
 
-        load_u_pair(0)
-        for g in range(BLOCKS // PAIR):
-            if g + 1 < BLOCKS // PAIR:
-                load_u_pair(g + 1)
-            if g == 0:
-                nc.sync.dma_start(offsets[:], offs)
-            for b in range(g * PAIR, (g + 1) * PAIR):
-                window = blocks.tile([P, S], F32, name="window")
-                nc.sync.dma_start(window[:], base[b * P : (b + 1) * P, :])
-                windows.append(window)
+        def load_window():
+            b = len(windows)
+            window = blocks.tile([P, S], F32, name="window")
+            nc.sync.dma_start(window[:], base[b * P : (b + 1) * P, :])
+            windows.append(window)
 
-        minus_ones = held.tile([E, P], BF16, name="minus_ones")
-        nc.vector.memset(minus_ones[:], -1.0)
-        twice_x = held.tile([E, N], BF16, name="twice_x")
-        nc.vector.tensor_scalar_mul(twice_x[:], x_sb[:], 2.0)
-        x_squared = held.tile([E, N], BF16, name="x_squared")
-        nc.vector.tensor_mul(x_squared[:], x_sb[:], x_sb[:])
-        squares = []
-        for b in range(BLOCKS):
-            centers_squared = blocks.tile([E, P], BF16, name="centers_squared")
-            nc.vector.tensor_mul(centers_squared[:], centers_blocks[b], centers_blocks[b])
-            squares.append(centers_squared)
+        nc.sync.dma_start(centers_first[:], centers[:, :FIRST])
+        nc.sync.dma_start(x_sb[:], x)
+        load_u(U_LOADS[0])
+        load_u(U_LOADS[1])
+        nc.sync.dma_start(centers_rest[:], centers[:, FIRST:])
+        load_u(U_LOADS[2])
+        nc.sync.dma_start(offsets[:], offs)
+        load_window()
+        load_window()
+        load_u(U_LOADS[3])
+        for b in range(2, BLOCKS):
+            load_window()
+
+        minus_halves = held.tile([E, P], BF16, name="minus_halves")
+        nc.vector.memset(minus_halves[:], -0.5)
+
+        def square(matrix, name):
+            squares = held.tile([E, P], BF16, name=name)
+            nc.vector.tensor_mul(squares[:], matrix, matrix)
+            return squares
+
+        centers_blocks = [centers_first[:]]
+        centers_blocks += [centers_rest[:, start : start + P] for start in range(0, K - FIRST, P)]
+        squares_blocks = [square(centers_blocks[0], "centers_squared_0")]
+        x_squared = square(x_sb[:], "x_squared")
+        for b in range(1, BLOCKS):
+            squares_blocks.append(square(centers_blocks[b], f"centers_squared_{b}"))
+
+        log_log_us = []
 
         def take_logs(b):
-            noise = noise_pairs[b // PAIR][:, b % PAIR, :]
-            nc.scalar.activation(noise, noise, LN)
-            nc.scalar.activation(noise, noise, LN, scale=-1.0)
+            log_log_u = ring.tile([P, N], F32, name="log_log_u")
+            nc.scalar.activation(log_log_u[:], u_blocks[b], LN)
+            nc.scalar.activation(log_log_u[:], log_log_u[:], LN, scale=-1.0)
+            log_log_us.append(log_log_u)
 
         for b in range(AHEAD):
             take_logs(b)
-
         for b in range(BLOCKS):
-            rows = slice(b * P, (b + 1) * P)
-            noise = noise_pairs[b // PAIR][:, b % PAIR, :]
-            window = windows[b]
             if b + AHEAD < BLOCKS:
                 take_logs(b + AHEAD)
-            nc.scalar.mul(noise, noise, -1.0)
+            noise = blocks.tile([P, N], F32, name="noise")
+            nc.scalar.mul(noise[:], log_log_us[b][:], -1.0)
 
-            negd = banks.tile([P, N], F32, name="negd")
-            nc.tensor.matmul(negd[:], minus_ones[:], x_squared[:], start=True, stop=False)
-            nc.tensor.matmul(negd[:], centers_blocks[b], twice_x[:], start=False, stop=False)
-            nc.tensor.matmul(negd[:], squares[b][:], minus_ones[:], start=False, stop=True)
-            negd_sb = blocks.tile([P, N], F32, name="negd_sb")
-            nc.scalar.copy(negd_sb[:], negd[:])
+            half_negd = banks.tile([P, N], F32, name="half_negd")
+            nc.tensor.matmul(half_negd[:], centers_blocks[b], x_sb[:], start=True, stop=False)
+            nc.tensor.matmul(half_negd[:], minus_halves[:], x_squared[:], start=False, stop=False)
+            nc.tensor.matmul(half_negd[:], squares_blocks[b][:], minus_halves[:], start=False, stop=True)
+            negd = u_blocks[b]
+            nc.scalar.mul(negd, half_negd[:], 2.0)
 
-            nc.vector.tensor_tensor(window[:].indirect(offsets[:]), negd_sb[:], noise, ADD)
-            nc.sync.dma_start(out[rows, :], window[:])
+            window = windows[b]
+            nc.vector.tensor_tensor(window[:].indirect(offsets[:]), negd, noise[:], ADD)
+            nc.sync.dma_start(out[b * P : (b + 1) * P, :], window[:])

@@ -4,7 +4,7 @@ K, E, S, N = 1024, 128, 256, 128
 P = 128
 BLOCKS = K // P
 U_LOADS = (1, 1, 2, 4)
-AHEAD = 1
+LOG_TILES = 2
 FIRST = P
 FLOPS = 2 * K * E * N
 
@@ -18,7 +18,6 @@ def tile_softclusteringmodule_kernel(tc, x, centers, u, base, offs, out):
     with (
         tc.tile_pool(name="held", bufs=1) as held,
         tc.tile_pool(name="blocks", bufs=BLOCKS) as blocks,
-        tc.tile_pool(name="ring", bufs=AHEAD + 1) as ring,
         tc.psum_pool(name="banks", bufs=2) as banks,
     ):
         x_sb = held.tile([E, N], BF16, name="x_sb")
@@ -40,14 +39,14 @@ def tile_softclusteringmodule_kernel(tc, x, centers, u, base, offs, out):
             nc.sync.dma_start(window[:], base[b * P : (b + 1) * P, :])
             windows.append(window)
 
+        load_u(U_LOADS[0])
         nc.sync.dma_start(centers_first[:], centers[:, :FIRST])
         nc.sync.dma_start(x_sb[:], x)
-        load_u(U_LOADS[0])
         load_u(U_LOADS[1])
         nc.sync.dma_start(centers_rest[:], centers[:, FIRST:])
-        load_u(U_LOADS[2])
         nc.sync.dma_start(offsets[:], offs)
         load_window()
+        load_u(U_LOADS[2])
         load_window()
         load_u(U_LOADS[3])
         for b in range(2, BLOCKS):
@@ -68,19 +67,24 @@ def tile_softclusteringmodule_kernel(tc, x, centers, u, base, offs, out):
         for b in range(1, BLOCKS):
             squares_blocks.append(square(centers_blocks[b], f"centers_squared_{b}"))
 
+        log_us = []
         log_log_us = []
 
         def take_logs(b):
-            log_log_u = ring.tile([P, N], F32, name="log_log_u")
-            nc.scalar.activation(log_log_u[:], u_blocks[b], LN)
-            nc.scalar.activation(log_log_u[:], log_log_u[:], LN, scale=-1.0)
+            if b < LOG_TILES:
+                log_u = blocks.tile([P, N], F32, name="log_u")
+            else:
+                log_u = log_log_us[b - LOG_TILES]
+            nc.scalar.activation(log_u[:], u_blocks[b], LN)
+            log_log_u = blocks.tile([P, N], F32, name="log_log_u")
+            nc.scalar.activation(log_log_u[:], log_u[:], LN, scale=-1.0)
+            log_us.append(log_u)
             log_log_us.append(log_log_u)
 
-        for b in range(AHEAD):
-            take_logs(b)
+        take_logs(0)
         for b in range(BLOCKS):
-            if b + AHEAD < BLOCKS:
-                take_logs(b + AHEAD)
+            if b + 1 < BLOCKS:
+                take_logs(b + 1)
             noise = blocks.tile([P, N], F32, name="noise")
             nc.scalar.mul(noise[:], log_log_us[b][:], -1.0)
 
@@ -88,9 +92,9 @@ def tile_softclusteringmodule_kernel(tc, x, centers, u, base, offs, out):
             nc.tensor.matmul(half_negd[:], centers_blocks[b], x_sb[:], start=True, stop=False)
             nc.tensor.matmul(half_negd[:], minus_halves[:], x_squared[:], start=False, stop=False)
             nc.tensor.matmul(half_negd[:], squares_blocks[b][:], minus_halves[:], start=False, stop=True)
-            negd = u_blocks[b]
-            nc.scalar.mul(negd, half_negd[:], 2.0)
+            negd = log_us[b]
+            nc.scalar.mul(negd[:], half_negd[:], 2.0)
 
             window = windows[b]
-            nc.vector.tensor_tensor(window[:].indirect(offsets[:]), negd, noise[:], ADD)
+            nc.vector.tensor_tensor(window[:].indirect(offsets[:]), negd[:], noise[:], ADD)
             nc.sync.dma_start(out[b * P : (b + 1) * P, :], window[:])

@@ -5,7 +5,7 @@ P = 128
 BLOCKS = K // P
 U_LOADS = (1, 1, 2, 4)
 LOG_TILES = 2
-FIRST = P
+FIRST = 2 * P
 FLOPS = 2 * K * E * N
 
 F32, BF16, U16 = mybir.dt.float32, mybir.dt.bfloat16, mybir.dt.uint16
@@ -60,7 +60,7 @@ def tile_softclusteringmodule_kernel(tc, x, centers, u, base, offs, out):
             nc.vector.tensor_mul(squares[:], matrix, matrix)
             return squares
 
-        centers_blocks = [centers_first[:]]
+        centers_blocks = [centers_first[:, start : start + P] for start in range(0, FIRST, P)]
         centers_blocks += [centers_rest[:, start : start + P] for start in range(0, K - FIRST, P)]
         squares_blocks = [square(centers_blocks[0], "centers_squared_0")]
         x_squared = square(x_sb[:], "x_squared")

@@ -40,8 +40,8 @@ def tile_softclusteringmodule_kernel(tc, x, centers, u, base, offs, out):
             windows.append(window)
 
         load_u(U_LOADS[0])
-        nc.sync.dma_start(centers_first[:], centers[:, :FIRST])
         nc.sync.dma_start(x_sb[:], x)
+        nc.sync.dma_start(centers_first[:], centers[:, :FIRST])
         load_u(U_LOADS[1])
         nc.sync.dma_start(centers_rest[:], centers[:, FIRST:])
         nc.sync.dma_start(offsets[:], offs)
@@ -62,10 +62,8 @@ def tile_softclusteringmodule_kernel(tc, x, centers, u, base, offs, out):
 
         centers_blocks = [centers_first[:, start : start + P] for start in range(0, FIRST, P)]
         centers_blocks += [centers_rest[:, start : start + P] for start in range(0, K - FIRST, P)]
-        squares_blocks = [square(centers_blocks[0], "centers_squared_0")]
         x_squared = square(x_sb[:], "x_squared")
-        for b in range(1, BLOCKS):
-            squares_blocks.append(square(centers_blocks[b], f"centers_squared_{b}"))
+        squares_blocks = [square(centers_blocks[b], f"centers_squared_{b}") for b in range(BLOCKS)]
 
         log_us = []
         log_log_us = []

import concourse.mybir as mybir

K, E, S, N = 1024, 128, 256, 128
P = 128
BLOCKS = K // P
U_LOADS = (1, 1, 2, 4)
LOG_TILES = 2
FIRST = 2 * P
FLOPS = 2 * K * E * N

F32, BF16, U16 = mybir.dt.float32, mybir.dt.bfloat16, mybir.dt.uint16
ADD = mybir.AluOpType.add
LN = mybir.ActivationFunctionType.Ln


def tile_softclusteringmodule_kernel(tc, x, centers, u, base, offs, out):
    nc = tc.nc
    with (
        tc.tile_pool(name="held", bufs=1) as held,
        tc.tile_pool(name="blocks", bufs=BLOCKS) as blocks,
        tc.psum_pool(name="banks", bufs=2) as banks,
    ):
        x_sb = held.tile([E, N], BF16, name="x_sb")
        centers_first = held.tile([E, FIRST], BF16, name="centers_first")
        centers_rest = held.tile([E, K - FIRST], BF16, name="centers_rest")
        offsets = held.tile([P, N // 16], U16, name="offsets")
        u_blocks = []
        windows = []

        def load_u(size):
            u_tile = held.tile([P, size, N], F32, name=f"u_{len(u_blocks)}")
            rows = u[len(u_blocks) * P : (len(u_blocks) + size) * P, :]
            nc.sync.dma_start(u_tile[:], rows.rearrange("(i p) j -> p i j", p=P))
            u_blocks.extend([u_tile[:, i, :] for i in range(size)])

        def load_window():
            b = len(windows)
            window = blocks.tile([P, S], F32, name="window")
            nc.sync.dma_start(window[:], base[b * P : (b + 1) * P, :])
            windows.append(window)

        load_u(U_LOADS[0])
        nc.sync.dma_start(x_sb[:], x)
        nc.sync.dma_start(centers_first[:], centers[:, :FIRST])
        load_u(U_LOADS[1])
        nc.sync.dma_start(centers_rest[:], centers[:, FIRST:])
        nc.sync.dma_start(offsets[:], offs)
        load_window()
        load_u(U_LOADS[2])
        load_window()
        load_u(U_LOADS[3])
        for b in range(2, BLOCKS):
            load_window()

        minus_halves = held.tile([E, P], BF16, name="minus_halves")
        nc.vector.memset(minus_halves[:], -0.5)

        def square(matrix, name):
            squares = held.tile([E, P], BF16, name=name)
            nc.vector.tensor_mul(squares[:], matrix, matrix)
            return squares

        centers_blocks = [centers_first[:, start : start + P] for start in range(0, FIRST, P)]
        centers_blocks += [centers_rest[:, start : start + P] for start in range(0, K - FIRST, P)]
        x_squared = square(x_sb[:], "x_squared")
        squares_blocks = [square(centers_blocks[b], f"centers_squared_{b}") for b in range(BLOCKS)]

        log_us = []
        log_log_us = []

        def take_logs(b):
            if b < LOG_TILES:
                log_u = blocks.tile([P, N], F32, name="log_u")
            else:
                log_u = log_log_us[b - LOG_TILES]
            nc.scalar.activation(log_u[:], u_blocks[b], LN)
            log_log_u = blocks.tile([P, N], F32, name="log_log_u")
            nc.scalar.activation(log_log_u[:], log_u[:], LN, scale=-1.0)
            log_us.append(log_u)
            log_log_us.append(log_log_u)

        take_logs(0)
        for b in range(BLOCKS):
            if b + 1 < BLOCKS:
                take_logs(b + 1)
            noise = blocks.tile([P, N], F32, name="noise")
            nc.scalar.mul(noise[:], log_log_us[b][:], -1.0)

            half_negd = banks.tile([P, N], F32, name="half_negd")
            nc.tensor.matmul(half_negd[:], centers_blocks[b], x_sb[:], start=True, stop=False)
            nc.tensor.matmul(half_negd[:], minus_halves[:], x_squared[:], start=False, stop=False)
            nc.tensor.matmul(half_negd[:], squares_blocks[b][:], minus_halves[:], start=False, stop=True)
            negd = log_us[b]
            nc.scalar.mul(negd[:], half_negd[:], 2.0)

            window = windows[b]
            nc.vector.tensor_tensor(window[:].indirect(offsets[:]), negd[:], noise[:], ADD)
            nc.sync.dma_start(out[b * P : (b + 1) * P, :], window[:])
